import numpy as np
import ml_dtypes


def mxq(x, axis, fmt="e4m3"):
    dtype, down = {"e4m3": (ml_dtypes.float8_e4m3fn, 7), "e5m2": (ml_dtypes.float8_e5m2, 14)}[fmt]
    v = np.moveaxis(np.asarray(x, np.float32).astype(ml_dtypes.bfloat16).astype(np.float64), axis, -1)
    blocks = v.reshape(v.shape[:-1] + (-1, 32))
    amax = np.abs(blocks).max(-1, keepdims=True)
    byte = np.maximum(np.where(amax > 0, np.frexp(amax)[1] - 1 + 127, 0) - down, 1)
    scale = np.exp2(byte - 127.0)
    codes = (blocks / scale).astype(np.float32).astype(dtype).astype(np.float64)
    return np.moveaxis((codes * scale).reshape(v.shape), -1, axis)


WIDE = False


def mx_kscale(k):
    if not WIDE:
        return np.ones(k)
    levels = np.array([10, -10, 5, -5, 0])
    a = np.random.permutation(np.resize(levels, k // 512 * 4)).reshape(k // 512, 4)
    idx = np.arange(k)
    return np.exp2(a[idx // 512, idx % 128 // 32])


BF16 = ml_dtypes.bfloat16


def bf(x):
    return np.asarray(x, np.float32).astype(BF16)


def f64(x):
    return np.asarray(x).astype(np.float64)


B, C, CI, N = 16, 256, 512, 512
EPS = 1e-5


def setup_inputs():
    s, t = mx_kscale(N), mx_kscale(CI)
    r = np.random.standard_normal
    return {"affinity": bf(r((B, N, N)) * 0.2 * s[None, None, :]),
            "g_x": bf(r((B, N, CI)) / s[None, :, None] * t[None, None, :]),
            "w_w": bf(r((C, CI)) * 1.5 / (0.2 * np.sqrt(N) * np.sqrt(CI)) / t[None, :]),
            "w_b": bf(r(C) * 0.3),
            "bn_gamma": bf(r(C)),
            "bn_beta": bf(r(C) * 0.5),
            "bn_mean": bf(r(C) * 0.5),
            "bn_var": bf(np.random.uniform(0.5, 1.5, C)),
            "x": bf(r((B, C, N)))}


def reference(affinity, g_x, w_w, w_b, bn_gamma, bn_beta, bn_mean, bn_var, x):
    y = (mxq(f64(affinity), 2, "e4m3") @ mxq(f64(g_x), 1, "e4m3")).transpose(0, 2, 1)
    wy = (mxq(f64(w_w), 1, "e4m3") @ mxq(y, 1, "e4m3")) + f64(w_b)[None, :, None]
    inv_std = 1.0 / np.sqrt(f64(bn_var) + EPS)
    wy = f64(bn_gamma)[None, :, None] * (wy - f64(bn_mean)[None, :, None]) * inv_std[None, :, None] + f64(bn_beta)[None, :, None]
    return wy + f64(x)

@@ -1,0 +1,277 @@
+from contextlib import ExitStack
+
+import concourse.mybir as mybir
+from concourse.masks import make_identity
+
+BF16 = mybir.dt.bfloat16
+F32 = mybir.dt.float32
+U32 = mybir.dt.uint32
+U8 = mybir.dt.uint8
+FP8X4 = mybir.dt.float8_e4m3fn_x4
+ALU = mybir.AluOpType
+ACT = mybir.ActivationFunctionType
+
+B, C, CI, N = 16, 256, 512, 512
+EPS = 1e-5
+FLOPS = 2 * B * (N * N * CI + C * CI * N)
+
+P = 128
+PACK = 4
+Q_TILES = N // P
+C_TILES = C // P
+
+LEAD = 3
+OPERANDS_AHEAD = 5
+RESIDUAL_AHEAD = 3
+RAW_BUFS = 6
+OUT_BUFS = 6
+
+
+def tile_sgcam_pb_t_kernel(
+    tc, affinity, g_x, w_w, w_b, bn_gamma, bn_beta, bn_mean, bn_var, x, out
+):
+    nc = tc.nc
+    with ExitStack() as ctx:
+        const = ctx.enter_context(tc.tile_pool(name="const", bufs=1))
+        raw = ctx.enter_context(tc.tile_pool(name="raw", bufs=RAW_BUFS))
+        work = ctx.enter_context(tc.tile_pool(name="work", bufs=2))
+        result = ctx.enter_context(tc.tile_pool(name="result", bufs=OUT_BUFS))
+        psum_a = ctx.enter_context(tc.psum_pool(name="psum_a", bufs=2))
+        psum_y = ctx.enter_context(tc.psum_pool(name="psum_y", bufs=Q_TILES))
+        psum_wy = ctx.enter_context(tc.psum_pool(name="psum_wy", bufs=C_TILES))
+        ctx.enter_context(tc.manual_schedule())
+
+        held = {}
+
+        def in_range(b):
+            return 0 <= b < B
+
+        def load_operands(b):
+            if not in_range(b):
+                return
+            g_raw = raw.tile([P, PACK, CI], BF16)
+            nc.sync.dma_start(
+                out=g_raw[:].rearrange("p (u e) c -> p u e c", u=2),
+                in_=g_x[b].rearrange("(u p e) c -> p u e c", u=2, e=2),
+            )
+            a_raw = raw.tile([P, PACK * N], BF16)
+            nc.sync.dma_start(
+                out=a_raw[:].rearrange("p (r s) -> p r s", r=PACK),
+                in_=affinity[b].rearrange("(p r) s -> p r s", r=PACK),
+            )
+            held["g_raw", b] = g_raw
+            held["a_raw", b] = a_raw
+
+        def load_residual(b):
+            if not in_range(b):
+                return
+            x_raw = raw.tile([P, C_TILES, N], BF16)
+            nc.sync.dma_start(out=x_raw[:], in_=x[b].rearrange("(p a) q -> p a q", a=C_TILES))
+            held["x_raw", b] = x_raw
+
+        def store(b):
+            if not in_range(b):
+                return
+            nc.sync.dma_start(
+                out=out[b].rearrange("(p a) q -> p a q", a=C_TILES), in_=held["result", b][:]
+            )
+
+        def transpose_affinity(b):
+            if not in_range(b):
+                return
+            a_words = held["a_raw", b][:].bitcast(F32)
+            for h in range(2):
+                a_t = psum_a.tile([P, 2, 2, P], F32)
+                for r in range(2):
+                    for u in range(2):
+                        first = (2 * h + r) * (N // 2) + u * P
+                        nc.tensor.transpose(
+                            a_t[:, r, u, :], a_words[:, first : first + P], ident_f32[:]
+                        )
+                held["a_t", b, h] = a_t
+
+        def regroup_affinity(b):
+            if not in_range(b):
+                return
+            a_grouped = work.tile([P, N * PACK], BF16, align_bytes=64)
+            words = a_grouped[:].bitcast(F32).rearrange("p (q r u) -> p q r u", r=PACK, u=2)
+            for h in range(2):
+                nc.scalar.copy(
+                    out=words[:, :, 2 * h : 2 * h + 2, :],
+                    in_=held["a_t", b, h][:].rearrange("p r u q -> p q r u"),
+                )
+            held["a_grouped", b] = a_grouped
+
+        def regroup_g(b):
+            if not in_range(b):
+                return
+            g_grouped = work.tile([P, CI * PACK], BF16, align_bytes=64)
+            nc.vector.tensor_copy(
+                out=g_grouped[:].rearrange("p (c i t) -> p c t i", i=4, t=PACK),
+                in_=held["g_raw", b][:].rearrange("p t (c i) -> p c t i", i=4),
+            )
+            held["g_grouped", b] = g_grouped
+
+        def quantise(what, b):
+            if not in_range(b):
+                return
+            codes = work.tile([P, N], U32, tag=what + "_codes", align_bytes=64)
+            scales = work.tile([P, N], U8, tag=what + "_scales", align_bytes=64)
+            nc.vector.quantize_mx(
+                out=codes[:].bitcast(FP8X4), scales=scales[:], in_=held[what + "_grouped", b][:]
+            )
+            held[what + "_codes", b] = codes
+            held[what + "_scales", b] = scales
+
+        def first_product(b, j):
+            if not in_range(b):
+                return
+            y_t = psum_y.tile([P, PACK, P], F32)
+            q_cols = slice(j * P, (j + 1) * P)
+            for t in range(PACK):
+                k_cols = slice(t * P, (t + 1) * P)
+                nc.tensor.matmul_mx(
+                    out=y_t[:, t, :],
+                    lhsT=held["g_codes", b][:, k_cols].bitcast(FP8X4),
+                    lhsT_scale=held["g_scales", b][:, k_cols],
+                    rhs=held["a_codes", b][:, q_cols].bitcast(FP8X4),
+                    rhs_scale=held["a_scales", b][:, q_cols],
+                    start=True,
+                    stop=True,
+                )
+            held["y_t", b, j] = y_t
+
+        def regroup_y(b, j):
+            if not in_range(b):
+                return
+            if j == 0:
+                y_grouped = work.tile([P, N * PACK], BF16, align_bytes=64)
+                held["y_grouped", b] = y_grouped
+            nc.scalar.copy(
+                out=held["y_grouped", b][:].rearrange("p (q t) -> p q t", t=PACK)[
+                    :, j * P : (j + 1) * P, :
+                ],
+                in_=held["y_t", b, j][:].rearrange("p t q -> p q t"),
+            )
+
+        def second_product(b):
+            if not in_range(b):
+                return
+            for a in range(C_TILES):
+                wy = psum_wy.tile([P, N], F32, tag="wy")
+                c_cols = slice(a * P, (a + 1) * P)
+                nc.tensor.matmul_mx(
+                    out=wy[:],
+                    lhsT=w_codes[:, c_cols].bitcast(FP8X4),
+                    lhsT_scale=w_scales[:, c_cols],
+                    rhs=held["y_codes", b][:].bitcast(FP8X4),
+                    rhs_scale=held["y_scales", b][:],
+                    start=True,
+                    stop=True,
+                )
+                held["wy", b, a] = wy
+
+        def shift_residual_on_scalar(b):
+            if not in_range(b):
+                return
+            res = result.tile([P, C_TILES, N], F32)
+            nc.scalar.activation(
+                out=res[:, 0, :],
+                in_=held["x_raw", b][:, 0, :],
+                func=ACT.Identity,
+                bias=shift[:, 0:1],
+                scale=1.0,
+            )
+            held["result", b] = res
+
+        def shift_residual_on_vector(b):
+            if not in_range(b):
+                return
+            nc.vector.tensor_scalar_add(
+                out=held["result", b][:, 1, :], in0=held["x_raw", b][:, 1, :], scalar1=shift[:, 1:2]
+            )
+
+        def finish(b):
+            if not in_range(b):
+                return
+            res = held["result", b]
+            for a in range(C_TILES):
+                nc.vector.scalar_tensor_tensor(
+                    out=res[:, a, :],
+                    in0=held["wy", b, a][:],
+                    scalar=scale[:, a : a + 1],
+                    in1=res[:, a, :],
+                    op0=ALU.mult,
+                    op1=ALU.add,
+                )
+
+        def step(i):
+            load_operands(i + OPERANDS_AHEAD)
+            load_residual(i + RESIDUAL_AHEAD)
+            regroup_g(i + 3)
+            shift_residual_on_vector(i)
+            for j in range(Q_TILES):
+                regroup_y(i, j)
+                first_product(i + 1, j)
+            quantise("y", i)
+            quantise("g", i + 2)
+            second_product(i)
+            regroup_affinity(i + 2)
+            transpose_affinity(i + 3)
+            shift_residual_on_scalar(i + 1)
+            finish(i)
+            quantise("a", i + 2)
+            store(i)
+
+        def load_vector(vector, name):
+            v = const.tile([P, C_TILES], BF16, name=name)
+            nc.scalar.dma_start(out=v[:], in_=vector.rearrange("(p a) -> p a", a=C_TILES))
+            return v
+
+        var = load_vector(bn_var, "var")
+        gamma = load_vector(bn_gamma, "gamma")
+        bias = load_vector(w_b, "bias")
+        mean = load_vector(bn_mean, "mean")
+        beta = load_vector(bn_beta, "beta")
+
+        for b in range(OPERANDS_AHEAD - LEAD):
+            load_operands(b)
+        w_raw = const.tile([P, C_TILES, CI], BF16)
+        nc.sync.dma_start(out=w_raw[:], in_=w_w.rearrange("(p a) k -> p a k", a=C_TILES))
+
+        ident_f32 = const.tile([P, P], F32)
+        make_identity(nc, ident_f32[:])
+        ident_bf16 = const.tile([P, P], BF16)
+        make_identity(nc, ident_bf16[:])
+
+        scale = const.tile([P, C_TILES], F32)
+        shift = const.tile([P, C_TILES], F32)
+        std = const.tile([P, C_TILES], F32)
+        nc.vector.tensor_scalar_add(out=std[:], in0=var[:], scalar1=EPS)
+        nc.scalar.sqrt(out=std[:], in_=std[:])
+        nc.vector.reciprocal(out=scale[:], in_=std[:])
+        nc.vector.tensor_mul(out=scale[:], in0=scale[:], in1=gamma[:])
+        nc.vector.tensor_sub(out=shift[:], in0=bias[:], in1=mean[:])
+        nc.vector.tensor_mul(out=shift[:], in0=shift[:], in1=scale[:])
+        nc.vector.tensor_add(out=shift[:], in0=shift[:], in1=beta[:])
+
+        for i in range(-LEAD, -1):
+            step(i)
+
+        w_t = psum_wy.tile([P, C_TILES, PACK, P], BF16, tag="wy")
+        for a in range(C_TILES):
+            for t in range(PACK):
+                nc.tensor.transpose(
+                    w_t[:, a, t, :], w_raw[:, a, t * P : (t + 1) * P], ident_bf16[:]
+                )
+        w_grouped = const.tile([P, C * PACK], BF16, align_bytes=64)
+        nc.scalar.copy(
+            out=w_grouped[:].rearrange("p (a c t) -> p a c t", a=C_TILES, t=PACK),
+            in_=w_t[:].rearrange("p a t c -> p a c t"),
+        )
+        w_codes = const.tile([P, C], U32, align_bytes=64)
+        w_scales = const.tile([P, C], U8, align_bytes=64)
+        nc.vector.quantize_mx(out=w_codes[:].bitcast(FP8X4), scales=w_scales[:], in_=w_grouped[:])
+
+        for i in range(-1, B):
+            step(i)

@@ -208,19 +208,19 @@ def tile_sgcam_pb_t_kernel(
         def step(i):
             load_operands(i + OPERANDS_AHEAD)
             load_residual(i + RESIDUAL_AHEAD)
-            regroup_g(i + 3)
-            shift_residual_on_vector(i)
             for j in range(Q_TILES):
                 regroup_y(i, j)
                 first_product(i + 1, j)
             quantise("y", i)
-            quantise("g", i + 2)
             second_product(i)
+            quantise("g", i + 2)
+            regroup_g(i + 3)
+            shift_residual_on_vector(i)
             regroup_affinity(i + 2)
             transpose_affinity(i + 3)
             shift_residual_on_scalar(i + 1)
-            finish(i)
             quantise("a", i + 2)
+            finish(i)
             store(i)
 
         def load_vector(vector, name):

@@ -184,11 +184,16 @@ def tile_sgcam_pb_t_kernel(
             )
             held["result", b] = res
 
-        def shift_residual_on_vector(b):
+        def shift_residual_on_gpsimd(b):
             if not in_range(b):
                 return
-            nc.vector.tensor_scalar_add(
-                out=held["result", b][:, 1, :], in0=held["x_raw", b][:, 1, :], scalar1=shift[:, 1:2]
+            nc.gpsimd.tensor_scalar(
+                out=held["result", b][:, 1, :],
+                in0=held["x_raw", b][:, 1, :],
+                scalar1=1.0,
+                scalar2=shift[:, 1:2],
+                op0=ALU.mult,
+                op1=ALU.add,
             )
 
         def finish(b):
@@ -215,10 +220,10 @@ def tile_sgcam_pb_t_kernel(
             second_product(i)
             quantise("g", i + 2)
             regroup_g(i + 3)
-            shift_residual_on_vector(i)
             regroup_affinity(i + 2)
             transpose_affinity(i + 3)
             shift_residual_on_scalar(i + 1)
+            shift_residual_on_gpsimd(i + 1)
             quantise("a", i + 2)
             finish(i)
             store(i)

@@ -21,10 +21,10 @@ Q_TILES = N // P
 C_TILES = C // P
 
 LEAD = 3
-OPERANDS_AHEAD = 5
-RESIDUAL_AHEAD = 3
-RAW_BUFS = 6
-OUT_BUFS = 6
+LOADS_AHEAD = 10
+RESIDUAL_LAG = 1
+RAW_BUFS = LOADS_AHEAD + 1
+OUT_BUFS = 8
 
 
 def tile_sgcam_pb_t_kernel(
@@ -46,7 +46,7 @@ def tile_sgcam_pb_t_kernel(
         def in_range(b):
             return 0 <= b < B
 
-        def load_operands(b):
+        def load_g(b):
             if not in_range(b):
                 return
             g_raw = raw.tile([P, PACK, CI], BF16)
@@ -54,12 +54,16 @@ def tile_sgcam_pb_t_kernel(
                 out=g_raw[:].rearrange("p (u e) c -> p u e c", u=2),
                 in_=g_x[b].rearrange("(u p e) c -> p u e c", u=2, e=2),
             )
+            held["g_raw", b] = g_raw
+
+        def load_affinity(b):
+            if not in_range(b):
+                return
             a_raw = raw.tile([P, PACK * N], BF16)
             nc.sync.dma_start(
                 out=a_raw[:].rearrange("p (r s) -> p r s", r=PACK),
                 in_=affinity[b].rearrange("(p r) s -> p r s", r=PACK),
             )
-            held["g_raw", b] = g_raw
             held["a_raw", b] = a_raw
 
         def load_residual(b):
@@ -68,6 +72,11 @@ def tile_sgcam_pb_t_kernel(
             x_raw = raw.tile([P, C_TILES, N], BF16)
             nc.sync.dma_start(out=x_raw[:], in_=x[b].rearrange("(p a) q -> p a q", a=C_TILES))
             held["x_raw", b] = x_raw
+
+        def load(b):
+            load_affinity(b)
+            load_g(b)
+            load_residual(b - RESIDUAL_LAG)
 
         def store(b):
             if not in_range(b):
@@ -211,22 +220,21 @@ def tile_sgcam_pb_t_kernel(
                 )
 
         def step(i):
-            load_operands(i + OPERANDS_AHEAD)
-            load_residual(i + RESIDUAL_AHEAD)
+            load(i + LOADS_AHEAD)
             for j in range(Q_TILES):
                 regroup_y(i, j)
                 first_product(i + 1, j)
             quantise("y", i)
+            finish(i - 1)
             second_product(i)
+            store(i - 1)
             quantise("g", i + 2)
-            regroup_g(i + 3)
             regroup_affinity(i + 2)
+            quantise("a", i + 2)
+            regroup_g(i + 3)
             transpose_affinity(i + 3)
             shift_residual_on_scalar(i + 1)
             shift_residual_on_gpsimd(i + 1)
-            quantise("a", i + 2)
-            finish(i)
-            store(i)
 
         def load_vector(vector, name):
             v = const.tile([P, C_TILES], BF16, name=name)
@@ -239,15 +247,15 @@ def tile_sgcam_pb_t_kernel(
         mean = load_vector(bn_mean, "mean")
         beta = load_vector(bn_beta, "beta")
 
-        for b in range(OPERANDS_AHEAD - LEAD):
-            load_operands(b)
         w_raw = const.tile([P, C_TILES, CI], BF16)
         nc.sync.dma_start(out=w_raw[:], in_=w_w.rearrange("(p a) k -> p a k", a=C_TILES))
+        for b in range(LOADS_AHEAD - LEAD):
+            load(b)
 
-        ident_f32 = const.tile([P, P], F32)
-        make_identity(nc, ident_f32[:])
         ident_bf16 = const.tile([P, P], BF16)
         make_identity(nc, ident_bf16[:])
+        ident_f32 = const.tile([P, P], F32)
+        make_identity(nc, ident_f32[:])
 
         scale = const.tile([P, C_TILES], F32)
         shift = const.tile([P, C_TILES], F32)
@@ -259,9 +267,6 @@ def tile_sgcam_pb_t_kernel(
         nc.vector.tensor_sub(out=shift[:], in0=bias[:], in1=mean[:])
         nc.vector.tensor_mul(out=shift[:], in0=shift[:], in1=scale[:])
         nc.vector.tensor_add(out=shift[:], in0=shift[:], in1=beta[:])
-
-        for i in range(-LEAD, -1):
-            step(i)
 
         w_t = psum_wy.tile([P, C_TILES, PACK, P], BF16, tag="wy")
         for a in range(C_TILES):
@@ -278,5 +283,5 @@ def tile_sgcam_pb_t_kernel(
         w_scales = const.tile([P, C], U8, align_bytes=64)
         nc.vector.quantize_mx(out=w_codes[:].bitcast(FP8X4), scales=w_scales[:], in_=w_grouped[:])
 
-        for i in range(-1, B):
+        for i in range(-LEAD, B + 1):
             step(i)

@@ -21,10 +21,11 @@ Q_TILES = N // P
 C_TILES = C // P
 
 LEAD = 3
-LOADS_AHEAD = 10
+LOADS_AHEAD = 8
 RESIDUAL_LAG = 1
 RAW_BUFS = LOADS_AHEAD + 1
-OUT_BUFS = 8
+OUT_BUFS = 10
+LAST_PIECES = 2
 
 
 def tile_sgcam_pb_t_kernel(
@@ -46,16 +47,6 @@ def tile_sgcam_pb_t_kernel(
         def in_range(b):
             return 0 <= b < B
 
-        def load_g(b):
-            if not in_range(b):
-                return
-            g_raw = raw.tile([P, PACK, CI], BF16)
-            nc.sync.dma_start(
-                out=g_raw[:].rearrange("p (u e) c -> p u e c", u=2),
-                in_=g_x[b].rearrange("(u p e) c -> p u e c", u=2, e=2),
-            )
-            held["g_raw", b] = g_raw
-
         def load_affinity(b):
             if not in_range(b):
                 return
@@ -65,6 +56,16 @@ def tile_sgcam_pb_t_kernel(
                 in_=affinity[b].rearrange("(p r) s -> p r s", r=PACK),
             )
             held["a_raw", b] = a_raw
+
+        def load_g(b):
+            if not in_range(b):
+                return
+            g_raw = raw.tile([P, PACK, CI], BF16)
+            nc.sync.dma_start(
+                out=g_raw[:].rearrange("p (u e) c -> p u e c", u=2),
+                in_=g_x[b].rearrange("(u p e) c -> p u e c", u=2, e=2),
+            )
+            held["g_raw", b] = g_raw
 
         def load_residual(b):
             if not in_range(b):
@@ -78,12 +79,15 @@ def tile_sgcam_pb_t_kernel(
             load_g(b)
             load_residual(b - RESIDUAL_LAG)
 
-        def store(b):
+        def regroup_g(b):
             if not in_range(b):
                 return
-            nc.sync.dma_start(
-                out=out[b].rearrange("(p a) q -> p a q", a=C_TILES), in_=held["result", b][:]
+            ag_grouped = work.tile([P, 2 * N * PACK], BF16, align_bytes=64)
+            nc.vector.tensor_copy(
+                out=ag_grouped[:, N * PACK :].rearrange("p (c i t) -> p c t i", i=4, t=PACK),
+                in_=held["g_raw", b][:].rearrange("p t (c i) -> p c t i", i=4),
             )
+            held["ag_grouped", b] = ag_grouped
 
         def transpose_affinity(b):
             if not in_range(b):
@@ -102,35 +106,27 @@ def tile_sgcam_pb_t_kernel(
         def regroup_affinity(b):
             if not in_range(b):
                 return
-            a_grouped = work.tile([P, N * PACK], BF16, align_bytes=64)
-            words = a_grouped[:].bitcast(F32).rearrange("p (q r u) -> p q r u", r=PACK, u=2)
+            words = (
+                held["ag_grouped", b][:, : N * PACK]
+                .bitcast(F32)
+                .rearrange("p (q r u) -> p q r u", r=PACK, u=2)
+            )
             for h in range(2):
                 nc.scalar.copy(
                     out=words[:, :, 2 * h : 2 * h + 2, :],
                     in_=held["a_t", b, h][:].rearrange("p r u q -> p q r u"),
                 )
-            held["a_grouped", b] = a_grouped
 
-        def regroup_g(b):
+        def quantise_operands(b):
             if not in_range(b):
                 return
-            g_grouped = work.tile([P, CI * PACK], BF16, align_bytes=64)
-            nc.vector.tensor_copy(
-                out=g_grouped[:].rearrange("p (c i t) -> p c t i", i=4, t=PACK),
-                in_=held["g_raw", b][:].rearrange("p t (c i) -> p c t i", i=4),
-            )
-            held["g_grouped", b] = g_grouped
-
-        def quantise(what, b):
-            if not in_range(b):
-                return
-            codes = work.tile([P, N], U32, tag=what + "_codes", align_bytes=64)
-            scales = work.tile([P, N], U8, tag=what + "_scales", align_bytes=64)
+            ag_codes = work.tile([P, 2 * N], U32, align_bytes=64)
+            ag_scales = work.tile([P, 2 * N], U8, align_bytes=64)
             nc.vector.quantize_mx(
-                out=codes[:].bitcast(FP8X4), scales=scales[:], in_=held[what + "_grouped", b][:]
+                out=ag_codes[:].bitcast(FP8X4), scales=ag_scales[:], in_=held["ag_grouped", b][:]
             )
-            held[what + "_codes", b] = codes
-            held[what + "_scales", b] = scales
+            held["ag_codes", b] = ag_codes
+            held["ag_scales", b] = ag_scales
 
         def first_product(b, j):
             if not in_range(b):
@@ -138,13 +134,13 @@ def tile_sgcam_pb_t_kernel(
             y_t = psum_y.tile([P, PACK, P], F32)
             q_cols = slice(j * P, (j + 1) * P)
             for t in range(PACK):
-                k_cols = slice(t * P, (t + 1) * P)
+                k_cols = slice(N + t * P, N + (t + 1) * P)
                 nc.tensor.matmul_mx(
                     out=y_t[:, t, :],
-                    lhsT=held["g_codes", b][:, k_cols].bitcast(FP8X4),
-                    lhsT_scale=held["g_scales", b][:, k_cols],
-                    rhs=held["a_codes", b][:, q_cols].bitcast(FP8X4),
-                    rhs_scale=held["a_scales", b][:, q_cols],
+                    lhsT=held["ag_codes", b][:, k_cols].bitcast(FP8X4),
+                    lhsT_scale=held["ag_scales", b][:, k_cols],
+                    rhs=held["ag_codes", b][:, q_cols].bitcast(FP8X4),
+                    rhs_scale=held["ag_scales", b][:, q_cols],
                     start=True,
                     stop=True,
                 )
@@ -163,24 +159,43 @@ def tile_sgcam_pb_t_kernel(
                 in_=held["y_t", b, j][:].rearrange("p t q -> p q t"),
             )
 
-        def second_product(b):
+        def pieces(b):
             if not in_range(b):
-                return
+                return []
+            count = LAST_PIECES if b == B - 1 else 1
+            width = N // count
+            return [(b, k * width, width) for k in range(count)]
+
+        def quantise_y(piece):
+            b, first, width = piece
+            if first == 0:
+                y_codes = work.tile([P, N], U32, align_bytes=64)
+                y_scales = work.tile([P, N], U8, align_bytes=64)
+                held["y_codes", b] = y_codes
+                held["y_scales", b] = y_scales
+            nc.vector.quantize_mx(
+                out=held["y_codes", b][:, first : first + width].bitcast(FP8X4),
+                scales=held["y_scales", b][:, first : first + width],
+                in_=held["y_grouped", b][:, first * PACK : (first + width) * PACK],
+            )
+
+        def second_product(piece):
+            b, first, width = piece
             for a in range(C_TILES):
-                wy = psum_wy.tile([P, N], F32, tag="wy")
+                wy = psum_wy.tile([P, width], F32, tag="wy")
                 c_cols = slice(a * P, (a + 1) * P)
                 nc.tensor.matmul_mx(
                     out=wy[:],
                     lhsT=w_codes[:, c_cols].bitcast(FP8X4),
                     lhsT_scale=w_scales[:, c_cols],
-                    rhs=held["y_codes", b][:].bitcast(FP8X4),
-                    rhs_scale=held["y_scales", b][:],
+                    rhs=held["y_codes", b][:, first : first + width].bitcast(FP8X4),
+                    rhs_scale=held["y_scales", b][:, first : first + width],
                     start=True,
                     stop=True,
                 )
-                held["wy", b, a] = wy
+                held["wy", piece, a] = wy
 
-        def shift_residual_on_scalar(b):
+        def shift_residual(b):
             if not in_range(b):
                 return
             res = result.tile([P, C_TILES, N], F32)
@@ -191,50 +206,49 @@ def tile_sgcam_pb_t_kernel(
                 bias=shift[:, 0:1],
                 scale=1.0,
             )
-            held["result", b] = res
-
-        def shift_residual_on_gpsimd(b):
-            if not in_range(b):
-                return
             nc.gpsimd.tensor_scalar(
-                out=held["result", b][:, 1, :],
+                out=res[:, 1, :],
                 in0=held["x_raw", b][:, 1, :],
                 scalar1=1.0,
                 scalar2=shift[:, 1:2],
                 op0=ALU.mult,
                 op1=ALU.add,
             )
+            held["result", b] = res
 
-        def finish(b):
-            if not in_range(b):
-                return
-            res = held["result", b]
+        def finish(piece):
+            b, first, width = piece
+            res = held["result", b][:, :, first : first + width]
             for a in range(C_TILES):
                 nc.vector.scalar_tensor_tensor(
                     out=res[:, a, :],
-                    in0=held["wy", b, a][:],
+                    in0=held["wy", piece, a][:],
                     scalar=scale[:, a : a + 1],
                     in1=res[:, a, :],
                     op0=ALU.mult,
                     op1=ALU.add,
                 )
+            nc.sync.dma_start(
+                out=out[b].rearrange("(p a) q -> p a q", a=C_TILES)[:, :, first : first + width],
+                in_=res,
+            )
 
         def step(i):
             load(i + LOADS_AHEAD)
             for j in range(Q_TILES):
                 regroup_y(i, j)
                 first_product(i + 1, j)
-            quantise("y", i)
-            finish(i - 1)
-            second_product(i)
-            store(i - 1)
-            quantise("g", i + 2)
+            for piece in pieces(i):
+                quantise_y(piece)
+                if held.get("unfinished"):
+                    finish(held["unfinished"])
+                second_product(piece)
+                held["unfinished"] = piece
             regroup_affinity(i + 2)
-            quantise("a", i + 2)
+            quantise_operands(i + 2)
             regroup_g(i + 3)
             transpose_affinity(i + 3)
-            shift_residual_on_scalar(i + 1)
-            shift_residual_on_gpsimd(i + 1)
+            shift_residual(i + 1)
 
         def load_vector(vector, name):
             v = const.tile([P, C_TILES], BF16, name=name)
@@ -283,5 +297,6 @@ def tile_sgcam_pb_t_kernel(
         w_scales = const.tile([P, C], U8, align_bytes=64)
         nc.vector.quantize_mx(out=w_codes[:].bitcast(FP8X4), scales=w_scales[:], in_=w_grouped[:])
 
-        for i in range(-LEAD, B + 1):
+        for i in range(-LEAD, B):
             step(i)
+        finish(held["unfinished"])

@@ -20,7 +20,7 @@ PACK = 4
 Q_TILES = N // P
 C_TILES = C // P
 
-LEAD = 3
+LEAD = 4
 LOADS_AHEAD = 8
 RESIDUAL_LAG = 1
 RAW_BUFS = LOADS_AHEAD + 1
@@ -36,6 +36,7 @@ def tile_sgcam_pb_t_kernel(
         const = ctx.enter_context(tc.tile_pool(name="const", bufs=1))
         raw = ctx.enter_context(tc.tile_pool(name="raw", bufs=RAW_BUFS))
         work = ctx.enter_context(tc.tile_pool(name="work", bufs=2))
+        grouped = ctx.enter_context(tc.tile_pool(name="grouped", bufs=3))
         result = ctx.enter_context(tc.tile_pool(name="result", bufs=OUT_BUFS))
         psum_a = ctx.enter_context(tc.psum_pool(name="psum_a", bufs=2))
         psum_y = ctx.enter_context(tc.psum_pool(name="psum_y", bufs=Q_TILES))
@@ -60,7 +61,7 @@ def tile_sgcam_pb_t_kernel(
         def load_g(b):
             if not in_range(b):
                 return
-            g_raw = raw.tile([P, PACK, CI], BF16)
+            g_raw = raw.tile([P, PACK, CI], BF16, tag="g_or_x_odd")
             nc.sync.dma_start(
                 out=g_raw[:].rearrange("p (u e) c -> p u e c", u=2),
                 in_=g_x[b].rearrange("(u p e) c -> p u e c", u=2, e=2),
@@ -75,14 +76,14 @@ def tile_sgcam_pb_t_kernel(
             held["x_raw", b] = x_raw
 
         def load(b):
-            load_affinity(b)
             load_g(b)
+            load_affinity(b)
             load_residual(b - RESIDUAL_LAG)
 
         def regroup_g(b):
             if not in_range(b):
                 return
-            ag_grouped = work.tile([P, 2 * N * PACK], BF16, align_bytes=64)
+            ag_grouped = grouped.tile([P, 2 * N * PACK], BF16, align_bytes=64)
             nc.vector.tensor_copy(
                 out=ag_grouped[:, N * PACK :].rearrange("p (c i t) -> p c t i", i=4, t=PACK),
                 in_=held["g_raw", b][:].rearrange("p t (c i) -> p c t i", i=4),
@@ -198,6 +199,7 @@ def tile_sgcam_pb_t_kernel(
         def shift_residual(b):
             if not in_range(b):
                 return
+            x_odd = raw.tile([P, N], F32, tag="g_or_x_odd")
             res = result.tile([P, C_TILES, N], F32)
             nc.scalar.activation(
                 out=res[:, 0, :],
@@ -207,7 +209,7 @@ def tile_sgcam_pb_t_kernel(
                 scale=1.0,
             )
             nc.gpsimd.tensor_scalar(
-                out=res[:, 1, :],
+                out=x_odd[:],
                 in0=held["x_raw", b][:, 1, :],
                 scalar1=1.0,
                 scalar2=shift[:, 1:2],
@@ -215,16 +217,18 @@ def tile_sgcam_pb_t_kernel(
                 op1=ALU.add,
             )
             held["result", b] = res
+            held["x_odd", b] = x_odd
 
         def finish(piece):
             b, first, width = piece
             res = held["result", b][:, :, first : first + width]
+            shifted = (res[:, 0, :], held["x_odd", b][:, first : first + width])
             for a in range(C_TILES):
                 nc.vector.scalar_tensor_tensor(
                     out=res[:, a, :],
                     in0=held["wy", piece, a][:],
                     scalar=scale[:, a : a + 1],
-                    in1=res[:, a, :],
+                    in1=shifted[a],
                     op0=ALU.mult,
                     op1=ALU.add,
                 )
@@ -246,7 +250,7 @@ def tile_sgcam_pb_t_kernel(
                 held["unfinished"] = piece
             regroup_affinity(i + 2)
             quantise_operands(i + 2)
-            regroup_g(i + 3)
+            regroup_g(i + 4)
             transpose_affinity(i + 3)
             shift_residual(i + 1)
 
@@ -261,26 +265,23 @@ def tile_sgcam_pb_t_kernel(
         mean = load_vector(bn_mean, "mean")
         beta = load_vector(bn_beta, "beta")
 
+        load_g(0)
+        load_affinity(0)
+        load_g(1)
         w_raw = const.tile([P, C_TILES, CI], BF16)
         nc.sync.dma_start(out=w_raw[:], in_=w_w.rearrange("(p a) k -> p a k", a=C_TILES))
-        for b in range(LOADS_AHEAD - LEAD):
+        load_affinity(1)
+        load_residual(0)
+        for b in range(2, LOADS_AHEAD - LEAD):
             load(b)
 
-        ident_bf16 = const.tile([P, P], BF16)
-        make_identity(nc, ident_bf16[:])
         ident_f32 = const.tile([P, P], F32)
         make_identity(nc, ident_f32[:])
+        ident_bf16 = const.tile([P, P], BF16)
+        make_identity(nc, ident_bf16[:])
 
-        scale = const.tile([P, C_TILES], F32)
-        shift = const.tile([P, C_TILES], F32)
-        std = const.tile([P, C_TILES], F32)
-        nc.vector.tensor_scalar_add(out=std[:], in0=var[:], scalar1=EPS)
-        nc.scalar.sqrt(out=std[:], in_=std[:])
-        nc.vector.reciprocal(out=scale[:], in_=std[:])
-        nc.vector.tensor_mul(out=scale[:], in0=scale[:], in1=gamma[:])
-        nc.vector.tensor_sub(out=shift[:], in0=bias[:], in1=mean[:])
-        nc.vector.tensor_mul(out=shift[:], in0=shift[:], in1=scale[:])
-        nc.vector.tensor_add(out=shift[:], in0=shift[:], in1=beta[:])
+        step(-4)
+        step(-3)
 
         w_t = psum_wy.tile([P, C_TILES, PACK, P], BF16, tag="wy")
         for a in range(C_TILES):
@@ -288,6 +289,22 @@ def tile_sgcam_pb_t_kernel(
                 nc.tensor.transpose(
                     w_t[:, a, t, :], w_raw[:, a, t * P : (t + 1) * P], ident_bf16[:]
                 )
+
+        scale = const.tile([P, C_TILES], F32)
+        shift = const.tile([P, C_TILES], F32)
+        std = const.tile([P, C_TILES], F32)
+        nc.gpsimd.tensor_scalar(
+            out=std[:], in0=var[:], scalar1=1.0, scalar2=EPS, op0=ALU.mult, op1=ALU.add
+        )
+        nc.scalar.sqrt(out=std[:], in_=std[:])
+        nc.vector.reciprocal(out=scale[:], in_=std[:])
+        nc.gpsimd.tensor_mul(out=scale[:], in0=scale[:], in1=gamma[:])
+        nc.gpsimd.tensor_sub(out=shift[:], in0=bias[:], in1=mean[:])
+        nc.gpsimd.tensor_mul(out=shift[:], in0=shift[:], in1=scale[:])
+        nc.gpsimd.tensor_add(out=shift[:], in0=shift[:], in1=beta[:])
+
+        step(-2)
+
         w_grouped = const.tile([P, C * PACK], BF16, align_bytes=64)
         nc.scalar.copy(
             out=w_grouped[:].rearrange("p (a c t) -> p a c t", a=C_TILES, t=PACK),
@@ -297,6 +314,6 @@ def tile_sgcam_pb_t_kernel(
         w_scales = const.tile([P, C], U8, align_bytes=64)
         nc.vector.quantize_mx(out=w_codes[:].bitcast(FP8X4), scales=w_scales[:], in_=w_grouped[:])
 
-        for i in range(-LEAD, B):
+        for i in range(-1, B):
             step(i)
         finish(held["unfinished"])

@@ -21,6 +21,7 @@ Q_TILES = N // P
 C_TILES = C // P
 
 LEAD = 4
+G_AHEAD = LEAD
 LOADS_AHEAD = 8
 RESIDUAL_LAG = 1
 RAW_BUFS = LOADS_AHEAD + 1
@@ -48,6 +49,9 @@ def tile_sgcam_pb_t_kernel(
         def in_range(b):
             return 0 <= b < B
 
+        def slot(b):
+            return f"slot{b % RAW_BUFS}"
+
         def load_affinity(b):
             if not in_range(b):
                 return
@@ -61,7 +65,7 @@ def tile_sgcam_pb_t_kernel(
         def load_g(b):
             if not in_range(b):
                 return
-            g_raw = raw.tile([P, PACK, CI], BF16, tag="g_or_x_odd")
+            g_raw = raw.tile([P, PACK, CI], BF16, tag=slot(b), bufs=1)
             nc.sync.dma_start(
                 out=g_raw[:].rearrange("p (u e) c -> p u e c", u=2),
                 in_=g_x[b].rearrange("(u p e) c -> p u e c", u=2, e=2),
@@ -199,7 +203,7 @@ def tile_sgcam_pb_t_kernel(
         def shift_residual(b):
             if not in_range(b):
                 return
-            x_odd = raw.tile([P, N], F32, tag="g_or_x_odd")
+            x_odd = raw.tile([P, N], F32, tag=slot(b - 1 + G_AHEAD), bufs=1)
             res = result.tile([P, C_TILES, N], F32)
             nc.scalar.activation(
                 out=res[:, 0, :],
@@ -250,7 +254,7 @@ def tile_sgcam_pb_t_kernel(
                 held["unfinished"] = piece
             regroup_affinity(i + 2)
             quantise_operands(i + 2)
-            regroup_g(i + 4)
+            regroup_g(i + G_AHEAD)
             transpose_affinity(i + 3)
             shift_residual(i + 1)
 

@@ -89,8 +89,8 @@ def tile_sgcam_pb_t_kernel(
                 return
             ag_grouped = grouped.tile([P, 2 * N * PACK], BF16, align_bytes=64)
             nc.vector.tensor_copy(
-                out=ag_grouped[:, N * PACK :].rearrange("p (c i t) -> p c t i", i=4, t=PACK),
-                in_=held["g_raw", b][:].rearrange("p t (c i) -> p c t i", i=4),
+                out=ag_grouped[:, N * PACK :].rearrange("p (c i t) -> p c t i", i=8, t=PACK),
+                in_=held["g_raw", b][:].rearrange("p t (c i) -> p c t i", i=8),
             )
             held["ag_grouped", b] = ag_grouped
 
@@ -186,11 +186,14 @@ def tile_sgcam_pb_t_kernel(
 
         def second_product(piece):
             b, first, width = piece
+            per_bank = 1 if width == N else C_TILES
             for a in range(C_TILES):
-                wy = psum_wy.tile([P, width], F32, tag="wy")
+                if a % per_bank == 0:
+                    bank = psum_wy.tile([P, per_bank, width], F32, tag="wy")
+                wy = bank[:, a % per_bank, :]
                 c_cols = slice(a * P, (a + 1) * P)
                 nc.tensor.matmul_mx(
-                    out=wy[:],
+                    out=wy,
                     lhsT=w_codes[:, c_cols].bitcast(FP8X4),
                     lhsT_scale=w_scales[:, c_cols],
                     rhs=held["y_codes", b][:, first : first + width].bitcast(FP8X4),
@@ -205,13 +208,18 @@ def tile_sgcam_pb_t_kernel(
                 return
             x_odd = raw.tile([P, N], F32, tag=slot(b - 1 + G_AHEAD), bufs=1)
             res = result.tile([P, C_TILES, N], F32)
-            nc.scalar.activation(
-                out=res[:, 0, :],
-                in_=held["x_raw", b][:, 0, :],
-                func=ACT.Identity,
-                bias=shift[:, 0:1],
-                scale=1.0,
-            )
+            if b >= B - 2:
+                nc.vector.tensor_scalar_add(
+                    out=res[:, 0, :], in0=held["x_raw", b][:, 0, :], scalar1=shift[:, 0:1]
+                )
+            else:
+                nc.scalar.activation(
+                    out=res[:, 0, :],
+                    in_=held["x_raw", b][:, 0, :],
+                    func=ACT.Identity,
+                    bias=shift[:, 0:1],
+                    scale=1.0,
+                )
             nc.gpsimd.tensor_scalar(
                 out=x_odd[:],
                 in0=held["x_raw", b][:, 1, :],
@@ -230,7 +238,7 @@ def tile_sgcam_pb_t_kernel(
             for a in range(C_TILES):
                 nc.vector.scalar_tensor_tensor(
                     out=res[:, a, :],
-                    in0=held["wy", piece, a][:],
+                    in0=held["wy", piece, a],
                     scalar=scale[:, a : a + 1],
                     in1=shifted[a],
                     op0=ALU.mult,
@@ -246,6 +254,8 @@ def tile_sgcam_pb_t_kernel(
             for j in range(Q_TILES):
                 regroup_y(i, j)
                 first_product(i + 1, j)
+            if i == B - 2:
+                finish(held.pop("unfinished"))
             for piece in pieces(i):
                 quantise_y(piece)
                 if held.get("unfinished"):

@@ -254,6 +254,8 @@ def tile_sgcam_pb_t_kernel(
             for j in range(Q_TILES):
                 regroup_y(i, j)
                 first_product(i + 1, j)
+            regroup_affinity(i + 2)
+            transpose_affinity(i + 3)
             if i == B - 2:
                 finish(held.pop("unfinished"))
             for piece in pieces(i):
@@ -262,10 +264,8 @@ def tile_sgcam_pb_t_kernel(
                     finish(held["unfinished"])
                 second_product(piece)
                 held["unfinished"] = piece
-            regroup_affinity(i + 2)
             quantise_operands(i + 2)
             regroup_g(i + G_AHEAD)
-            transpose_affinity(i + 3)
             shift_residual(i + 1)
 
         def load_vector(vector, name):

@@ -20,13 +20,17 @@ PACK = 4
 Q_TILES = N // P
 C_TILES = C // P
 
-LEAD = 4
+LEAD = 3
 G_AHEAD = LEAD
 LOADS_AHEAD = 8
-RESIDUAL_LAG = 1
+RESIDUAL_LAG = 2
+SCALAR_CHANNELS = 32
+SHARED_FROM = 4
+RUN = 8
 RAW_BUFS = LOADS_AHEAD + 1
 OUT_BUFS = 10
 LAST_PIECES = 2
+EARLY = ((0, 0), (0, 1))
 
 
 def tile_sgcam_pb_t_kernel(
@@ -88,10 +92,17 @@ def tile_sgcam_pb_t_kernel(
             if not in_range(b):
                 return
             ag_grouped = grouped.tile([P, 2 * N * PACK], BF16, align_bytes=64)
-            nc.vector.tensor_copy(
-                out=ag_grouped[:, N * PACK :].rearrange("p (c i t) -> p c t i", i=8, t=PACK),
-                in_=held["g_raw", b][:].rearrange("p t (c i) -> p c t i", i=8),
-            )
+            cut = CI - (SCALAR_CHANNELS if b >= SHARED_FROM else 0)
+            for copy, first, end in ((nc.vector.tensor_copy, 0, cut), (nc.scalar.copy, cut, CI)):
+                if first < end:
+                    copy(
+                        out=ag_grouped[:, (N + first) * PACK : (N + end) * PACK].rearrange(
+                            "p (c i t) -> p c t i", i=RUN, t=PACK
+                        ),
+                        in_=held["g_raw", b][:, :, first:end].rearrange(
+                            "p t (c i) -> p c t i", i=RUN
+                        ),
+                    )
             held["ag_grouped", b] = ag_grouped
 
         def transpose_affinity(b):
@@ -203,23 +214,10 @@ def tile_sgcam_pb_t_kernel(
                 )
                 held["wy", piece, a] = wy
 
-        def shift_residual(b):
+        def shift_residual_odd(b):
             if not in_range(b):
                 return
             x_odd = raw.tile([P, N], F32, tag=slot(b - 1 + G_AHEAD), bufs=1)
-            res = result.tile([P, C_TILES, N], F32)
-            if b >= B - 2:
-                nc.vector.tensor_scalar_add(
-                    out=res[:, 0, :], in0=held["x_raw", b][:, 0, :], scalar1=shift[:, 0:1]
-                )
-            else:
-                nc.scalar.activation(
-                    out=res[:, 0, :],
-                    in_=held["x_raw", b][:, 0, :],
-                    func=ACT.Identity,
-                    bias=shift[:, 0:1],
-                    scale=1.0,
-                )
             nc.gpsimd.tensor_scalar(
                 out=x_odd[:],
                 in0=held["x_raw", b][:, 1, :],
@@ -228,8 +226,20 @@ def tile_sgcam_pb_t_kernel(
                 op0=ALU.mult,
                 op1=ALU.add,
             )
-            held["result", b] = res
             held["x_odd", b] = x_odd
+
+        def shift_residual_even(b):
+            if not in_range(b):
+                return
+            res = result.tile([P, C_TILES, N], F32)
+            nc.scalar.activation(
+                out=res[:, 0, :],
+                in_=held["x_raw", b][:, 0, :],
+                func=ACT.Identity,
+                bias=shift[:, 0:1],
+                scale=1.0,
+            )
+            held["result", b] = res
 
         def finish(piece):
             b, first, width = piece
@@ -252,11 +262,15 @@ def tile_sgcam_pb_t_kernel(
         def step(i):
             load(i + LOADS_AHEAD)
             for j in range(Q_TILES):
-                regroup_y(i, j)
+                if (i, j) not in EARLY:
+                    regroup_y(i, j)
                 first_product(i + 1, j)
             regroup_affinity(i + 2)
             transpose_affinity(i + 3)
+            if i < B - 1:
+                shift_residual_even(i)
             if i == B - 2:
+                shift_residual_even(B - 1)
                 finish(held.pop("unfinished"))
             for piece in pieces(i):
                 quantise_y(piece)
@@ -266,7 +280,7 @@ def tile_sgcam_pb_t_kernel(
                 held["unfinished"] = piece
             quantise_operands(i + 2)
             regroup_g(i + G_AHEAD)
-            shift_residual(i + 1)
+            shift_residual_odd(i + 1)
 
         def load_vector(vector, name):
             v = const.tile([P, C_TILES], BF16, name=name)
@@ -279,30 +293,19 @@ def tile_sgcam_pb_t_kernel(
         mean = load_vector(bn_mean, "mean")
         beta = load_vector(bn_beta, "beta")
 
-        load_g(0)
         load_affinity(0)
-        load_g(1)
+        load_g(0)
         w_raw = const.tile([P, C_TILES, CI], BF16)
         nc.sync.dma_start(out=w_raw[:], in_=w_w.rearrange("(p a) k -> p a k", a=C_TILES))
+        load_g(1)
         load_affinity(1)
-        load_residual(0)
-        for b in range(2, LOADS_AHEAD - LEAD):
+        for b in range(2, LOADS_AHEAD):
             load(b)
 
         ident_f32 = const.tile([P, P], F32)
         make_identity(nc, ident_f32[:])
         ident_bf16 = const.tile([P, P], BF16)
         make_identity(nc, ident_bf16[:])
-
-        step(-4)
-        step(-3)
-
-        w_t = psum_wy.tile([P, C_TILES, PACK, P], BF16, tag="wy")
-        for a in range(C_TILES):
-            for t in range(PACK):
-                nc.tensor.transpose(
-                    w_t[:, a, t, :], w_raw[:, a, t * P : (t + 1) * P], ident_bf16[:]
-                )
 
         scale = const.tile([P, C_TILES], F32)
         shift = const.tile([P, C_TILES], F32)
@@ -311,23 +314,46 @@ def tile_sgcam_pb_t_kernel(
             out=std[:], in0=var[:], scalar1=1.0, scalar2=EPS, op0=ALU.mult, op1=ALU.add
         )
         nc.scalar.sqrt(out=std[:], in_=std[:])
-        nc.vector.reciprocal(out=scale[:], in_=std[:])
-        nc.gpsimd.tensor_mul(out=scale[:], in0=scale[:], in1=gamma[:])
-        nc.gpsimd.tensor_sub(out=shift[:], in0=bias[:], in1=mean[:])
-        nc.gpsimd.tensor_mul(out=shift[:], in0=shift[:], in1=scale[:])
-        nc.gpsimd.tensor_add(out=shift[:], in0=shift[:], in1=beta[:])
 
-        step(-2)
+        transpose_affinity(0)
+        regroup_g(0)
+        regroup_affinity(0)
+        quantise_operands(0)
 
+        w_t = psum_wy.tile([P, C_TILES, PACK, P], BF16, tag="wy")
+        for a in range(C_TILES):
+            for t in range(PACK):
+                nc.tensor.transpose(
+                    w_t[:, a, t, :], w_raw[:, a, t * P : (t + 1) * P], ident_bf16[:]
+                )
         w_grouped = const.tile([P, C * PACK], BF16, align_bytes=64)
         nc.scalar.copy(
             out=w_grouped[:].rearrange("p (a c t) -> p a c t", a=C_TILES, t=PACK),
             in_=w_t[:].rearrange("p a t c -> p a c t"),
         )
+
+        for j in range(Q_TILES):
+            first_product(0, j)
+        for b, j in EARLY:
+            regroup_y(b, j)
+
+        regroup_g(1)
+        nc.vector.reciprocal(out=scale[:], in_=std[:])
+        nc.gpsimd.tensor_mul(out=scale[:], in0=scale[:], in1=gamma[:])
+        nc.gpsimd.tensor_sub(out=shift[:], in0=bias[:], in1=mean[:])
+        nc.gpsimd.tensor_mul(out=shift[:], in0=shift[:], in1=scale[:])
+        nc.gpsimd.tensor_add(out=shift[:], in0=shift[:], in1=beta[:])
         w_codes = const.tile([P, C], U32, align_bytes=64)
         w_scales = const.tile([P, C], U8, align_bytes=64)
         nc.vector.quantize_mx(out=w_codes[:].bitcast(FP8X4), scales=w_scales[:], in_=w_grouped[:])
 
-        for i in range(-1, B):
+        transpose_affinity(1)
+        regroup_affinity(1)
+        regroup_g(2)
+        quantise_operands(1)
+        transpose_affinity(2)
+        shift_residual_odd(0)
+
+        for i in range(B):
             step(i)
         finish(held["unfinished"])

from contextlib import ExitStack

import concourse.mybir as mybir
from concourse.masks import make_identity

BF16 = mybir.dt.bfloat16
F32 = mybir.dt.float32
U32 = mybir.dt.uint32
U8 = mybir.dt.uint8
FP8X4 = mybir.dt.float8_e4m3fn_x4
ALU = mybir.AluOpType
ACT = mybir.ActivationFunctionType

B, C, CI, N = 16, 256, 512, 512
EPS = 1e-5
FLOPS = 2 * B * (N * N * CI + C * CI * N)

P = 128
PACK = 4
Q_TILES = N // P
C_TILES = C // P

LEAD = 3
G_AHEAD = LEAD
LOADS_AHEAD = 8
RESIDUAL_LAG = 2
SCALAR_CHANNELS = 32
SHARED_FROM = 4
RUN = 8
RAW_BUFS = LOADS_AHEAD + 1
OUT_BUFS = 10
LAST_PIECES = 2
EARLY = ((0, 0), (0, 1))


def tile_sgcam_pb_t_kernel(
    tc, affinity, g_x, w_w, w_b, bn_gamma, bn_beta, bn_mean, bn_var, x, out
):
    nc = tc.nc
    with ExitStack() as ctx:
        const = ctx.enter_context(tc.tile_pool(name="const", bufs=1))
        raw = ctx.enter_context(tc.tile_pool(name="raw", bufs=RAW_BUFS))
        work = ctx.enter_context(tc.tile_pool(name="work", bufs=2))
        grouped = ctx.enter_context(tc.tile_pool(name="grouped", bufs=3))
        result = ctx.enter_context(tc.tile_pool(name="result", bufs=OUT_BUFS))
        psum_a = ctx.enter_context(tc.psum_pool(name="psum_a", bufs=2))
        psum_y = ctx.enter_context(tc.psum_pool(name="psum_y", bufs=Q_TILES))
        psum_wy = ctx.enter_context(tc.psum_pool(name="psum_wy", bufs=C_TILES))
        ctx.enter_context(tc.manual_schedule())

        held = {}

        def in_range(b):
            return 0 <= b < B

        def slot(b):
            return f"slot{b % RAW_BUFS}"

        def load_affinity(b):
            if not in_range(b):
                return
            a_raw = raw.tile([P, PACK * N], BF16)
            nc.sync.dma_start(
                out=a_raw[:].rearrange("p (r s) -> p r s", r=PACK),
                in_=affinity[b].rearrange("(p r) s -> p r s", r=PACK),
            )
            held["a_raw", b] = a_raw

        def load_g(b):
            if not in_range(b):
                return
            g_raw = raw.tile([P, PACK, CI], BF16, tag=slot(b), bufs=1)
            nc.sync.dma_start(
                out=g_raw[:].rearrange("p (u e) c -> p u e c", u=2),
                in_=g_x[b].rearrange("(u p e) c -> p u e c", u=2, e=2),
            )
            held["g_raw", b] = g_raw

        def load_residual(b):
            if not in_range(b):
                return
            x_raw = raw.tile([P, C_TILES, N], BF16)
            nc.sync.dma_start(out=x_raw[:], in_=x[b].rearrange("(p a) q -> p a q", a=C_TILES))
            held["x_raw", b] = x_raw

        def load(b):
            load_g(b)
            load_affinity(b)
            load_residual(b - RESIDUAL_LAG)

        def regroup_g(b):
            if not in_range(b):
                return
            ag_grouped = grouped.tile([P, 2 * N * PACK], BF16, align_bytes=64)
            cut = CI - (SCALAR_CHANNELS if b >= SHARED_FROM else 0)
            for copy, first, end in ((nc.vector.tensor_copy, 0, cut), (nc.scalar.copy, cut, CI)):
                if first < end:
                    copy(
                        out=ag_grouped[:, (N + first) * PACK : (N + end) * PACK].rearrange(
                            "p (c i t) -> p c t i", i=RUN, t=PACK
                        ),
                        in_=held["g_raw", b][:, :, first:end].rearrange(
                            "p t (c i) -> p c t i", i=RUN
                        ),
                    )
            held["ag_grouped", b] = ag_grouped

        def transpose_affinity(b):
            if not in_range(b):
                return
            a_words = held["a_raw", b][:].bitcast(F32)
            for h in range(2):
                a_t = psum_a.tile([P, 2, 2, P], F32)
                for r in range(2):
                    for u in range(2):
                        first = (2 * h + r) * (N // 2) + u * P
                        nc.tensor.transpose(
                            a_t[:, r, u, :], a_words[:, first : first + P], ident_f32[:]
                        )
                held["a_t", b, h] = a_t

        def regroup_affinity(b):
            if not in_range(b):
                return
            words = (
                held["ag_grouped", b][:, : N * PACK]
                .bitcast(F32)
                .rearrange("p (q r u) -> p q r u", r=PACK, u=2)
            )
            for h in range(2):
                nc.scalar.copy(
                    out=words[:, :, 2 * h : 2 * h + 2, :],
                    in_=held["a_t", b, h][:].rearrange("p r u q -> p q r u"),
                )

        def quantise_operands(b):
            if not in_range(b):
                return
            ag_codes = work.tile([P, 2 * N], U32, align_bytes=64)
            ag_scales = work.tile([P, 2 * N], U8, align_bytes=64)
            nc.vector.quantize_mx(
                out=ag_codes[:].bitcast(FP8X4), scales=ag_scales[:], in_=held["ag_grouped", b][:]
            )
            held["ag_codes", b] = ag_codes
            held["ag_scales", b] = ag_scales

        def first_product(b, j):
            if not in_range(b):
                return
            y_t = psum_y.tile([P, PACK, P], F32)
            q_cols = slice(j * P, (j + 1) * P)
            for t in range(PACK):
                k_cols = slice(N + t * P, N + (t + 1) * P)
                nc.tensor.matmul_mx(
                    out=y_t[:, t, :],
                    lhsT=held["ag_codes", b][:, k_cols].bitcast(FP8X4),
                    lhsT_scale=held["ag_scales", b][:, k_cols],
                    rhs=held["ag_codes", b][:, q_cols].bitcast(FP8X4),
                    rhs_scale=held["ag_scales", b][:, q_cols],
                    start=True,
                    stop=True,
                )
            held["y_t", b, j] = y_t

        def regroup_y(b, j):
            if not in_range(b):
                return
            if j == 0:
                y_grouped = work.tile([P, N * PACK], BF16, align_bytes=64)
                held["y_grouped", b] = y_grouped
            nc.scalar.copy(
                out=held["y_grouped", b][:].rearrange("p (q t) -> p q t", t=PACK)[
                    :, j * P : (j + 1) * P, :
                ],
                in_=held["y_t", b, j][:].rearrange("p t q -> p q t"),
            )

        def pieces(b):
            if not in_range(b):
                return []
            count = LAST_PIECES if b == B - 1 else 1
            width = N // count
            return [(b, k * width, width) for k in range(count)]

        def quantise_y(piece):
            b, first, width = piece
            if first == 0:
                y_codes = work.tile([P, N], U32, align_bytes=64)
                y_scales = work.tile([P, N], U8, align_bytes=64)
                held["y_codes", b] = y_codes
                held["y_scales", b] = y_scales
            nc.vector.quantize_mx(
                out=held["y_codes", b][:, first : first + width].bitcast(FP8X4),
                scales=held["y_scales", b][:, first : first + width],
                in_=held["y_grouped", b][:, first * PACK : (first + width) * PACK],
            )

        def second_product(piece):
            b, first, width = piece
            per_bank = 1 if width == N else C_TILES
            for a in range(C_TILES):
                if a % per_bank == 0:
                    bank = psum_wy.tile([P, per_bank, width], F32, tag="wy")
                wy = bank[:, a % per_bank, :]
                c_cols = slice(a * P, (a + 1) * P)
                nc.tensor.matmul_mx(
                    out=wy,
                    lhsT=w_codes[:, c_cols].bitcast(FP8X4),
                    lhsT_scale=w_scales[:, c_cols],
                    rhs=held["y_codes", b][:, first : first + width].bitcast(FP8X4),
                    rhs_scale=held["y_scales", b][:, first : first + width],
                    start=True,
                    stop=True,
                )
                held["wy", piece, a] = wy

        def shift_residual_odd(b):
            if not in_range(b):
                return
            x_odd = raw.tile([P, N], F32, tag=slot(b - 1 + G_AHEAD), bufs=1)
            nc.gpsimd.tensor_scalar(
                out=x_odd[:],
                in0=held["x_raw", b][:, 1, :],
                scalar1=1.0,
                scalar2=shift[:, 1:2],
                op0=ALU.mult,
                op1=ALU.add,
            )
            held["x_odd", b] = x_odd

        def shift_residual_even(b):
            if not in_range(b):
                return
            res = result.tile([P, C_TILES, N], F32)
            nc.scalar.activation(
                out=res[:, 0, :],
                in_=held["x_raw", b][:, 0, :],
                func=ACT.Identity,
                bias=shift[:, 0:1],
                scale=1.0,
            )
            held["result", b] = res

        def finish(piece):
            b, first, width = piece
            res = held["result", b][:, :, first : first + width]
            shifted = (res[:, 0, :], held["x_odd", b][:, first : first + width])
            for a in range(C_TILES):
                nc.vector.scalar_tensor_tensor(
                    out=res[:, a, :],
                    in0=held["wy", piece, a],
                    scalar=scale[:, a : a + 1],
                    in1=shifted[a],
                    op0=ALU.mult,
                    op1=ALU.add,
                )
            nc.sync.dma_start(
                out=out[b].rearrange("(p a) q -> p a q", a=C_TILES)[:, :, first : first + width],
                in_=res,
            )

        def step(i):
            load(i + LOADS_AHEAD)
            for j in range(Q_TILES):
                if (i, j) not in EARLY:
                    regroup_y(i, j)
                first_product(i + 1, j)
            regroup_affinity(i + 2)
            transpose_affinity(i + 3)
            if i < B - 1:
                shift_residual_even(i)
            if i == B - 2:
                shift_residual_even(B - 1)
                finish(held.pop("unfinished"))
            for piece in pieces(i):
                quantise_y(piece)
                if held.get("unfinished"):
                    finish(held["unfinished"])
                second_product(piece)
                held["unfinished"] = piece
            quantise_operands(i + 2)
            regroup_g(i + G_AHEAD)
            shift_residual_odd(i + 1)

        def load_vector(vector, name):
            v = const.tile([P, C_TILES], BF16, name=name)
            nc.scalar.dma_start(out=v[:], in_=vector.rearrange("(p a) -> p a", a=C_TILES))
            return v

        var = load_vector(bn_var, "var")
        gamma = load_vector(bn_gamma, "gamma")
        bias = load_vector(w_b, "bias")
        mean = load_vector(bn_mean, "mean")
        beta = load_vector(bn_beta, "beta")

        load_affinity(0)
        load_g(0)
        w_raw = const.tile([P, C_TILES, CI], BF16)
        nc.sync.dma_start(out=w_raw[:], in_=w_w.rearrange("(p a) k -> p a k", a=C_TILES))
        load_g(1)
        load_affinity(1)
        for b in range(2, LOADS_AHEAD):
            load(b)

        ident_f32 = const.tile([P, P], F32)
        make_identity(nc, ident_f32[:])
        ident_bf16 = const.tile([P, P], BF16)
        make_identity(nc, ident_bf16[:])

        scale = const.tile([P, C_TILES], F32)
        shift = const.tile([P, C_TILES], F32)
        std = const.tile([P, C_TILES], F32)
        nc.gpsimd.tensor_scalar(
            out=std[:], in0=var[:], scalar1=1.0, scalar2=EPS, op0=ALU.mult, op1=ALU.add
        )
        nc.scalar.sqrt(out=std[:], in_=std[:])

        transpose_affinity(0)
        regroup_g(0)
        regroup_affinity(0)
        quantise_operands(0)

        w_t = psum_wy.tile([P, C_TILES, PACK, P], BF16, tag="wy")
        for a in range(C_TILES):
            for t in range(PACK):
                nc.tensor.transpose(
                    w_t[:, a, t, :], w_raw[:, a, t * P : (t + 1) * P], ident_bf16[:]
                )
        w_grouped = const.tile([P, C * PACK], BF16, align_bytes=64)
        nc.scalar.copy(
            out=w_grouped[:].rearrange("p (a c t) -> p a c t", a=C_TILES, t=PACK),
            in_=w_t[:].rearrange("p a t c -> p a c t"),
        )

        for j in range(Q_TILES):
            first_product(0, j)
        for b, j in EARLY:
            regroup_y(b, j)

        regroup_g(1)
        nc.vector.reciprocal(out=scale[:], in_=std[:])
        nc.gpsimd.tensor_mul(out=scale[:], in0=scale[:], in1=gamma[:])
        nc.gpsimd.tensor_sub(out=shift[:], in0=bias[:], in1=mean[:])
        nc.gpsimd.tensor_mul(out=shift[:], in0=shift[:], in1=scale[:])
        nc.gpsimd.tensor_add(out=shift[:], in0=shift[:], in1=beta[:])
        w_codes = const.tile([P, C], U32, align_bytes=64)
        w_scales = const.tile([P, C], U8, align_bytes=64)
        nc.vector.quantize_mx(out=w_codes[:].bitcast(FP8X4), scales=w_scales[:], in_=w_grouped[:])

        transpose_affinity(1)
        regroup_affinity(1)
        regroup_g(2)
        quantise_operands(1)
        transpose_affinity(2)
        shift_residual_odd(0)

        for i in range(B):
            step(i)
        finish(held["unfinished"])
